import numpy as np
import ml_dtypes


def mxq(x, axis, fmt="e4m3"):
    dtype, down = {"e4m3": (ml_dtypes.float8_e4m3fn, 7), "e5m2": (ml_dtypes.float8_e5m2, 14)}[fmt]
    v = np.moveaxis(np.asarray(x, np.float32).astype(ml_dtypes.bfloat16).astype(np.float64), axis, -1)
    blocks = v.reshape(v.shape[:-1] + (-1, 32))
    amax = np.abs(blocks).max(-1, keepdims=True)
    byte = np.maximum(np.where(amax > 0, np.frexp(amax)[1] - 1 + 127, 0) - down, 1)
    scale = np.exp2(byte - 127.0)
    codes = (blocks / scale).astype(np.float32).astype(dtype).astype(np.float64)
    return np.moveaxis((codes * scale).reshape(v.shape), -1, axis)


WIDE = False


def mx_kscale(k):
    if not WIDE:
        return np.ones(k)
    levels = np.array([10, -10, 5, -5, 0])
    a = np.random.permutation(np.resize(levels, k // 512 * 4)).reshape(k // 512, 4)
    idx = np.arange(k)
    return np.exp2(a[idx // 512, idx % 128 // 32])


BF16 = ml_dtypes.bfloat16


def bf(x):
    return np.asarray(x, np.float32).astype(BF16)


def f64(x):
    return np.asarray(x).astype(np.float64)


B, N, F = 32, 512, 128


def setup_inputs():
    s = mx_kscale(N)
    return {"regional_means": bf(np.random.standard_normal((B, N, F)) * (4.0 / np.sqrt(N)) / s[:, None]),
            "adj": bf(np.random.uniform(0.0, 1.0, (B, N, N)) * s)}


def reference(regional_means, adj):
    n = adj.shape[-1]
    mask = 1.0 - np.eye(n)
    adj_masked = f64(adj) * mask
    return mxq(adj_masked, 2, "e4m3") @ mxq(f64(regional_means), 1, "e4m3")

@@ -1,0 +1,186 @@
+from contextlib import ExitStack
+
+import concourse.mybir as mybir
+from concourse.masks import make_identity
+
+FP8X4 = mybir.dt.float8_e4m3fn_x4
+BF16 = mybir.dt.bfloat16
+F32 = mybir.dt.float32
+U32 = mybir.dt.uint32
+U8 = mybir.dt.uint8
+MULT = mybir.AluOpType.mult
+ADD = mybir.AluOpType.add
+
+B, N, F, P = 32, 512, 128, 128
+FLOPS = 2 * B * N * N * F
+
+STORE_LAG = 12
+ADJ_BUFS = STORE_LAG + 2
+OUT_BUFS = 9
+
+
+def tile_gcn_kernel(tc, regional_means, adj, out):
+    nc = tc.nc
+    with ExitStack() as ctx:
+        const = ctx.enter_context(tc.tile_pool(name="const", bufs=1))
+        adj_pool = ctx.enter_context(tc.tile_pool(name="adjp", bufs=ADJ_BUFS))
+        r_pool = ctx.enter_context(tc.tile_pool(name="rp", bufs=B // 2))
+        rg_pool = ctx.enter_context(tc.tile_pool(name="rgp", bufs=3))
+        rc_pool = ctx.enter_context(tc.tile_pool(name="rcp", bufs=5))
+        g_pool = ctx.enter_context(tc.tile_pool(name="gp", bufs=3))
+        c_pool = ctx.enter_context(tc.tile_pool(name="cp", bufs=3))
+        o_pool = ctx.enter_context(tc.tile_pool(name="op", bufs=OUT_BUFS))
+        pt_pool = ctx.enter_context(tc.psum_pool(name="ptp", bufs=6))
+        po_pool = ctx.enter_context(tc.psum_pool(name="pop", bufs=2))
+        ctx.enter_context(tc.manual_schedule())
+
+        ident = const.tile([P, P], F32, name="ident")
+        make_identity(nc, ident[:])
+        not_eye = const.tile([P, P], BF16, name="not_eye")
+        nc.vector.tensor_scalar(out=not_eye[:], in0=ident[:], scalar1=-1.0, scalar2=1.0, op0=MULT, op1=ADD)
+
+        adj_sb = {}
+        r_raw = {}
+        r_grp = {}
+        r_codes = {}
+        r_scales = {}
+        banks = {}
+        grouped = {}
+        a_codes = {}
+        a_scales = {}
+        o_ps = {}
+        o_sb = {}
+
+        def load_adj(b):
+            t = adj_pool.tile([P, 4 * N], BF16, name="adj_sb")
+            adj_sb[b] = t
+            nc.sync.dma_start(
+                out=t[:].rearrange("p (t j) -> p t j", t=4),
+                in_=adj[b].rearrange("(t p) j -> p t j", p=P),
+            )
+
+        def load_r(g):
+            t = r_pool.tile([P, 2, 4, F], BF16, name="r_raw")
+            r_raw[g] = t
+            nc.sync.dma_start(
+                out=t[:].rearrange("q b (u e) f -> q (b u) (e f)", u=2),
+                in_=regional_means[2 * g : 2 * g + 2].rearrange("b (u q e) f -> q (b u) (e f)", u=2, q=P, e=2),
+            )
+
+        def regroup_r(b):
+            rg = rg_pool.tile([P, F, 4], BF16, name="r_grp", align_bytes=64)
+            r_grp[b] = rg
+            nc.vector.tensor_copy(
+                out=rg[:].rearrange("q (c i) v -> q c v i", i=4),
+                in_=r_raw[b // 2][:, b % 2].rearrange("q v (c i) -> q c v i", i=4),
+            )
+
+        def quantise_r(b):
+            rc = rc_pool.tile([P, F], U32, name="r_codes", align_bytes=64)
+            rs = rc_pool.tile([P, F], U8, name="r_scales", align_bytes=64)
+            r_codes[b] = rc
+            r_scales[b] = rs
+            nc.vector.quantize_mx(
+                out=rc[:].bitcast(FP8X4), scales=rs[:], in_=r_grp[b][:].rearrange("q f v -> q (f v)")
+            )
+
+        def mask(b):
+            d = adj_sb[b][:].rearrange("p (g c) -> p g c", c=P)[:, 0:16:5, :]
+            nc.vector.tensor_tensor(
+                out=d, in0=d, in1=not_eye[:].unsqueeze(1).to_broadcast([P, 4, P]), op=MULT
+            )
+
+        def transposes(b):
+            words = adj_sb[b][:].bitcast(F32)
+            for h in range(2):
+                pt = pt_pool.tile([P, 2, 2, P], F32, name="pt")
+                banks[(b, h)] = pt
+                for u in range(2):
+                    for tp in range(2):
+                        c0 = 256 * (2 * h + tp) + 128 * u
+                        nc.tensor.transpose(pt[:, u, tp, :], words[:, c0 : c0 + 128], ident[:])
+
+        def exits(b):
+            g = g_pool.tile([P, 4 * N], BF16, name="grouped", align_bytes=64)
+            grouped[b] = g
+            gw = g[:].bitcast(F32).rearrange("p (T M u) -> p T M u", T=4, u=2)
+            for h in range(2):
+                nc.scalar.copy(
+                    out=gw[:, :, 64 * h : 64 * h + 64, :],
+                    in_=banks[(b, h)][:].rearrange("p u t (m T) -> p T (t m) u", T=4),
+                )
+
+        def quantise_a(b):
+            ac = c_pool.tile([P, N], U32, name="a_codes", align_bytes=64)
+            sc = c_pool.tile([P, N], U8, name="a_scales", align_bytes=64)
+            a_codes[b] = ac
+            a_scales[b] = sc
+            nc.vector.quantize_mx(out=ac[:].bitcast(FP8X4), scales=sc[:], in_=grouped[b][:])
+
+        def multiply(b):
+            po = po_pool.tile([P, 4, F], F32, name="po")
+            o_ps[b] = po
+            for T in range(4):
+                rows = slice(P * T, P * T + P)
+                nc.tensor.matmul_mx(
+                    out=po[:, T, :],
+                    lhsT=a_codes[b][:, rows].bitcast(FP8X4),
+                    lhsT_scale=a_scales[b][:, rows],
+                    rhs=r_codes[b][:].bitcast(FP8X4),
+                    rhs_scale=r_scales[b][:],
+                    start=True,
+                    stop=True,
+                )
+
+        def out_exit(b):
+            if b % 2 == 0:
+                o_sb[b // 2] = o_pool.tile([P, 2, 4, F], F32, name="o_sb")
+            nc.scalar.copy(out=o_sb[b // 2][:, b % 2], in_=o_ps[b][:])
+
+        def store(g):
+            nc.sync.dma_start(
+                out=out[2 * g : 2 * g + 2].rearrange("b (m T) f -> m b (T f)", T=4),
+                in_=o_sb[g][:].rearrange("m b T f -> m b (T f)"),
+            )
+
+        loads = []
+        for b in range(B):
+            tick = max(b - STORE_LAG, -1)
+            loads.append(("a", b, tick))
+            if b == 0:
+                loads.append(("r", 0, tick))
+            if b % 2 == 1 and b // 2 + 1 < B // 2:
+                loads.append(("r", b // 2 + 1, tick))
+
+        def issue_loads(now):
+            for kind, idx, tick in loads:
+                if tick == now and kind == "a":
+                    load_adj(idx)
+                if tick == now and kind == "r":
+                    load_r(idx)
+
+        issue_loads(-1)
+        mask(0)
+        regroup_r(0)
+        regroup_r(1)
+        quantise_r(0)
+        for i in range(B + 1):
+            if i >= 1:
+                quantise_a(i - 1)
+            if i + 1 < B:
+                mask(i + 1)
+            if i + 2 < B:
+                regroup_r(i + 2)
+            if i + 1 < B:
+                quantise_r(i + 1)
+            if i < B:
+                transposes(i)
+            if i >= 1:
+                multiply(i - 1)
+            if i < B:
+                exits(i)
+            if i >= 1:
+                out_exit(i - 1)
+                if (i - 1) % 2 == 1:
+                    store((i - 1) // 2)
+            issue_loads(i)

@@ -15,7 +15,7 @@ B, N, F, P = 32, 512, 128, 128
 FLOPS = 2 * B * N * N * F
 
 STORE_LAG = 12
-ADJ_BUFS = STORE_LAG + 2
+ADJ_BUFS = STORE_LAG // 2 + 2
 OUT_BUFS = 9
 
 
@@ -36,8 +36,16 @@ def tile_gcn_kernel(tc, regional_means, adj, out):
 
         ident = const.tile([P, P], F32, name="ident")
         make_identity(nc, ident[:])
-        not_eye = const.tile([P, P], BF16, name="not_eye")
-        nc.vector.tensor_scalar(out=not_eye[:], in0=ident[:], scalar1=-1.0, scalar2=1.0, op0=MULT, op1=ADD)
+        perm = const.tile([P, P], F32, name="perm")
+        nc.vector.tensor_copy(
+            out=perm[:].rearrange("p (mm m) -> p mm m", mm=2), in_=ident[:].rearrange("p (m mm) -> p mm m", mm=2)
+        )
+        keep = const.tile([P, 2, P, 2], BF16, name="keep")
+        nc.vector.memset(keep[:], 1.0)
+        for t in range(2):
+            nc.vector.tensor_scalar(
+                out=keep[:, t, :, t], in0=ident[:], scalar1=-1.0, scalar2=1.0, op0=MULT, op1=ADD
+            )
 
         adj_sb = {}
         r_raw = {}
@@ -51,12 +59,12 @@ def tile_gcn_kernel(tc, regional_means, adj, out):
         o_ps = {}
         o_sb = {}
 
-        def load_adj(b):
-            t = adj_pool.tile([P, 4 * N], BF16, name="adj_sb")
-            adj_sb[b] = t
+        def load_adj(g):
+            t = adj_pool.tile([P, 2, 4 * N], BF16, name="adj_sb")
+            adj_sb[g] = t
             nc.sync.dma_start(
-                out=t[:].rearrange("p (t j) -> p t j", t=4),
-                in_=adj[b].rearrange("(t p) j -> p t j", p=P),
+                out=t[:].rearrange("p b (h x) -> p (b h) x", h=2),
+                in_=adj[2 * g : 2 * g + 2].rearrange("b (h p t) j -> p (b h) (t j)", h=2, t=2),
             )
 
         def load_r(g):
@@ -84,30 +92,35 @@ def tile_gcn_kernel(tc, regional_means, adj, out):
                 out=rc[:].bitcast(FP8X4), scales=rs[:], in_=r_grp[b][:].rearrange("q f v -> q (f v)")
             )
 
-        def mask(b):
-            d = adj_sb[b][:].rearrange("p (g c) -> p g c", c=P)[:, 0:16:5, :]
-            nc.vector.tensor_tensor(
-                out=d, in0=d, in1=not_eye[:].unsqueeze(1).to_broadcast([P, 4, P]), op=MULT
-            )
+        def mask(g):
+            v = adj_sb[g][:].rearrange("p b (h t k c) -> p b h t k c", h=2, t=2, k=2)
+            for h in range(2):
+                d = v[:, :, h, :, h, :]
+                nc.vector.tensor_tensor(
+                    out=d,
+                    in0=d,
+                    in1=keep[:].rearrange("p t m e -> p t (m e)").unsqueeze(1).to_broadcast([P, 2, 2, 2 * P]),
+                    op=MULT,
+                )
 
         def transposes(b):
-            words = adj_sb[b][:].bitcast(F32)
+            words = adj_sb[b // 2][:, b % 2].bitcast(F32)
             for h in range(2):
                 pt = pt_pool.tile([P, 2, 2, P], F32, name="pt")
                 banks[(b, h)] = pt
                 for u in range(2):
-                    for tp in range(2):
-                        c0 = 256 * (2 * h + tp) + 128 * u
-                        nc.tensor.transpose(pt[:, u, tp, :], words[:, c0 : c0 + 128], ident[:])
+                    for t in range(2):
+                        c0 = 256 * (2 * h + t) + 128 * u
+                        nc.tensor.transpose(pt[:, u, t, :], words[:, c0 : c0 + 128], perm[:])
 
         def exits(b):
             g = g_pool.tile([P, 4 * N], BF16, name="grouped", align_bytes=64)
             grouped[b] = g
-            gw = g[:].bitcast(F32).rearrange("p (T M u) -> p T M u", T=4, u=2)
+            gw = g[:].bitcast(F32).rearrange("p (s M u) -> p s M u", s=4, u=2)
             for h in range(2):
                 nc.scalar.copy(
                     out=gw[:, :, 64 * h : 64 * h + 64, :],
-                    in_=banks[(b, h)][:].rearrange("p u t (m T) -> p T (t m) u", T=4),
+                    in_=banks[(b, h)][:].rearrange("p u t (mm m) -> p (t mm) m u", mm=2),
                 )
 
         def quantise_a(b):
@@ -120,17 +133,19 @@ def tile_gcn_kernel(tc, regional_means, adj, out):
         def multiply(b):
             po = po_pool.tile([P, 4, F], F32, name="po")
             o_ps[b] = po
-            for T in range(4):
-                rows = slice(P * T, P * T + P)
-                nc.tensor.matmul_mx(
-                    out=po[:, T, :],
-                    lhsT=a_codes[b][:, rows].bitcast(FP8X4),
-                    lhsT_scale=a_scales[b][:, rows],
-                    rhs=r_codes[b][:].bitcast(FP8X4),
-                    rhs_scale=r_scales[b][:],
-                    start=True,
-                    stop=True,
-                )
+            for t in range(2):
+                for mm in range(2):
+                    s = 2 * t + mm
+                    rows = slice(P * s, P * s + P)
+                    nc.tensor.matmul_mx(
+                        out=po[:, 2 * mm + t, :],
+                        lhsT=a_codes[b][:, rows].bitcast(FP8X4),
+                        lhsT_scale=a_scales[b][:, rows],
+                        rhs=r_codes[b][:].bitcast(FP8X4),
+                        rhs_scale=r_scales[b][:],
+                        start=True,
+                        stop=True,
+                    )
 
         def out_exit(b):
             if b % 2 == 0:
@@ -144,13 +159,13 @@ def tile_gcn_kernel(tc, regional_means, adj, out):
             )
 
         loads = []
-        for b in range(B):
-            tick = max(b - STORE_LAG, -1)
-            loads.append(("a", b, tick))
-            if b == 0:
+        for g in range(B // 2):
+            tick = max(2 * g - STORE_LAG, -1)
+            loads.append(("a", g, tick))
+            if g == 0:
                 loads.append(("r", 0, tick))
-            if b % 2 == 1 and b // 2 + 1 < B // 2:
-                loads.append(("r", b // 2 + 1, tick))
+            if g + 1 < B // 2:
+                loads.append(("r", g + 1, tick))
 
         def issue_loads(now):
             for kind, idx, tick in loads:
@@ -167,8 +182,8 @@ def tile_gcn_kernel(tc, regional_means, adj, out):
         for i in range(B + 1):
             if i >= 1:
                 quantise_a(i - 1)
-            if i + 1 < B:
-                mask(i + 1)
+            if i % 2 == 1 and i + 1 < B:
+                mask((i + 1) // 2)
             if i + 2 < B:
                 regroup_r(i + 2)
             if i + 1 < B:

@@ -14,9 +14,9 @@ ADD = mybir.AluOpType.add
 B, N, F, P = 32, 512, 128, 128
 FLOPS = 2 * B * N * N * F
 
-STORE_LAG = 12
-ADJ_BUFS = STORE_LAG // 2 + 2
-OUT_BUFS = 9
+STORE_LAG = 20
+ADJ_BUFS = STORE_LAG // 2 + 1
+OUT_BUFS = 13
 
 
 def tile_gcn_kernel(tc, regional_means, adj, out):
@@ -26,9 +26,9 @@ def tile_gcn_kernel(tc, regional_means, adj, out):
         adj_pool = ctx.enter_context(tc.tile_pool(name="adjp", bufs=ADJ_BUFS))
         r_pool = ctx.enter_context(tc.tile_pool(name="rp", bufs=B // 2))
         rg_pool = ctx.enter_context(tc.tile_pool(name="rgp", bufs=3))
-        rc_pool = ctx.enter_context(tc.tile_pool(name="rcp", bufs=5))
-        g_pool = ctx.enter_context(tc.tile_pool(name="gp", bufs=3))
-        c_pool = ctx.enter_context(tc.tile_pool(name="cp", bufs=3))
+        rc_pool = ctx.enter_context(tc.tile_pool(name="rcp", bufs=6))
+        g_pool = ctx.enter_context(tc.tile_pool(name="gp", bufs=4))
+        c_pool = ctx.enter_context(tc.tile_pool(name="cp", bufs=4))
         o_pool = ctx.enter_context(tc.tile_pool(name="op", bufs=OUT_BUFS))
         pt_pool = ctx.enter_context(tc.psum_pool(name="ptp", bufs=6))
         po_pool = ctx.enter_context(tc.psum_pool(name="pop", bufs=2))
@@ -179,23 +179,23 @@ def tile_gcn_kernel(tc, regional_means, adj, out):
         regroup_r(0)
         regroup_r(1)
         quantise_r(0)
-        for i in range(B + 1):
-            if i >= 1:
-                quantise_a(i - 1)
+        for i in range(B + 2):
             if i % 2 == 1 and i + 1 < B:
                 mask((i + 1) // 2)
+            if 1 <= i <= B:
+                quantise_a(i - 1)
             if i + 2 < B:
                 regroup_r(i + 2)
             if i + 1 < B:
                 quantise_r(i + 1)
             if i < B:
                 transposes(i)
-            if i >= 1:
-                multiply(i - 1)
+            if i >= 2:
+                multiply(i - 2)
             if i < B:
                 exits(i)
-            if i >= 1:
-                out_exit(i - 1)
-                if (i - 1) % 2 == 1:
-                    store((i - 1) // 2)
+            if i >= 2:
+                out_exit(i - 2)
+                if i % 2 == 1:
+                    store((i - 2) // 2)
             issue_loads(i)

@@ -71,8 +71,8 @@ def tile_gcn_kernel(tc, regional_means, adj, out):
             t = r_pool.tile([P, 2, 4, F], BF16, name="r_raw")
             r_raw[g] = t
             nc.sync.dma_start(
-                out=t[:].rearrange("q b (u e) f -> q (b u) (e f)", u=2),
-                in_=regional_means[2 * g : 2 * g + 2].rearrange("b (u q e) f -> q (b u) (e f)", u=2, q=P, e=2),
+                out=t[:].rearrange("q b v f -> q b (v f)"),
+                in_=regional_means[2 * g : 2 * g + 2].rearrange("b (q v) f -> q b (v f)", v=4),
             )
 
         def regroup_r(b):
@@ -110,8 +110,8 @@ def tile_gcn_kernel(tc, regional_means, adj, out):
                 banks[(b, h)] = pt
                 for u in range(2):
                     for t in range(2):
-                        c0 = 256 * (2 * h + t) + 128 * u
-                        nc.tensor.transpose(pt[:, u, t, :], words[:, c0 : c0 + 128], perm[:])
+                        c0 = 256 * (2 * h + t)
+                        nc.tensor.transpose(pt[:, u, t, :], words[:, c0 + u : c0 + 256 : 2], perm[:])
 
         def exits(b):
             g = g_pool.tile([P, 4 * N], BF16, name="grouped", align_bytes=64)

@@ -24,7 +24,8 @@ def tile_gcn_kernel(tc, regional_means, adj, out):
     with ExitStack() as ctx:
         const = ctx.enter_context(tc.tile_pool(name="const", bufs=1))
         adj_pool = ctx.enter_context(tc.tile_pool(name="adjp", bufs=ADJ_BUFS))
-        r_pool = ctx.enter_context(tc.tile_pool(name="rp", bufs=B // 2))
+        cm_pool = ctx.enter_context(tc.tile_pool(name="cmp", bufs=3))
+        r_pool = ctx.enter_context(tc.tile_pool(name="rp", bufs=13))
         rg_pool = ctx.enter_context(tc.tile_pool(name="rgp", bufs=3))
         rc_pool = ctx.enter_context(tc.tile_pool(name="rcp", bufs=6))
         g_pool = ctx.enter_context(tc.tile_pool(name="gp", bufs=4))
@@ -36,10 +37,6 @@ def tile_gcn_kernel(tc, regional_means, adj, out):
 
         ident = const.tile([P, P], F32, name="ident")
         make_identity(nc, ident[:])
-        perm = const.tile([P, P], F32, name="perm")
-        nc.vector.tensor_copy(
-            out=perm[:].rearrange("p (mm m) -> p mm m", mm=2), in_=ident[:].rearrange("p (m mm) -> p mm m", mm=2)
-        )
         keep = const.tile([P, 2, P, 2], BF16, name="keep")
         nc.vector.memset(keep[:], 1.0)
         for t in range(2):
@@ -48,6 +45,7 @@ def tile_gcn_kernel(tc, regional_means, adj, out):
             )
 
         adj_sb = {}
+        masked = {}
         r_raw = {}
         r_grp = {}
         r_codes = {}
@@ -62,10 +60,7 @@ def tile_gcn_kernel(tc, regional_means, adj, out):
         def load_adj(g):
             t = adj_pool.tile([P, 2, 4 * N], BF16, name="adj_sb")
             adj_sb[g] = t
-            nc.sync.dma_start(
-                out=t[:].rearrange("p b (h x) -> p (b h) x", h=2),
-                in_=adj[2 * g : 2 * g + 2].rearrange("b (h p t) j -> p (b h) (t j)", h=2, t=2),
-            )
+            nc.sync.dma_start(out=t[:], in_=adj[2 * g : 2 * g + 2].rearrange("b (p T) j -> p b (T j)", T=4))
 
         def load_r(g):
             t = r_pool.tile([P, 2, 4, F], BF16, name="r_raw")
@@ -93,34 +88,38 @@ def tile_gcn_kernel(tc, regional_means, adj, out):
             )
 
         def mask(g):
-            v = adj_sb[g][:].rearrange("p b (h t k c) -> p b h t k c", h=2, t=2, k=2)
-            for h in range(2):
-                d = v[:, :, h, :, h, :]
+            cm = cm_pool.tile([P, 2, 2, N], BF16, name="masked")
+            masked[g] = cm
+            for s in range(2):
                 nc.vector.tensor_tensor(
-                    out=d,
-                    in0=d,
-                    in1=keep[:].rearrange("p t m e -> p t (m e)").unsqueeze(1).to_broadcast([P, 2, 2, 2 * P]),
+                    out=cm[:, :, s, :].rearrange("p b (n e) -> p b n e", e=2),
+                    in0=adj_sb[g][:, :, 2 * N * s : 2 * N * s + 2 * N].rearrange("p b (n w) -> p b n w", w=4)[
+                        :, :, :, 2 * s : 2 * s + 2
+                    ],
+                    in1=keep[:].rearrange("p t q e -> p (t q) e").unsqueeze(1).to_broadcast([P, 2, 2 * P, 2]),
                     op=MULT,
                 )
 
         def transposes(b):
             words = adj_sb[b // 2][:, b % 2].bitcast(F32)
+            mwords = masked[b // 2][:, b % 2].rearrange("p s x -> p (s x)").bitcast(F32)
             for h in range(2):
                 pt = pt_pool.tile([P, 2, 2, P], F32, name="pt")
                 banks[(b, h)] = pt
-                for u in range(2):
-                    for t in range(2):
-                        c0 = 256 * (2 * h + t)
-                        nc.tensor.transpose(pt[:, u, t, :], words[:, c0 + u : c0 + 256 : 2], perm[:])
+                for t in range(2):
+                    c0 = 256 * (2 * h + t)
+                    nc.tensor.transpose(pt[:, 1 - h, t, :], words[:, c0 + 1 - h : c0 + 256 : 2], ident[:])
+                for t in range(2):
+                    c0 = 256 * h + 128 * t
+                    nc.tensor.transpose(pt[:, h, t, :], mwords[:, c0 : c0 + 128], ident[:])
 
         def exits(b):
             g = g_pool.tile([P, 4 * N], BF16, name="grouped", align_bytes=64)
             grouped[b] = g
-            gw = g[:].bitcast(F32).rearrange("p (s M u) -> p s M u", s=4, u=2)
+            gw = g[:].bitcast(F32).rearrange("p (T m s) -> p T m s", T=4, s=2)
             for h in range(2):
                 nc.scalar.copy(
-                    out=gw[:, :, 64 * h : 64 * h + 64, :],
-                    in_=banks[(b, h)][:].rearrange("p u t (mm m) -> p (t mm) m u", mm=2),
+                    out=gw[:, 2 * h : 2 * h + 2, :, :], in_=banks[(b, h)][:].rearrange("p s t m -> p t m s")
                 )
 
         def quantise_a(b):
@@ -133,19 +132,17 @@ def tile_gcn_kernel(tc, regional_means, adj, out):
         def multiply(b):
             po = po_pool.tile([P, 4, F], F32, name="po")
             o_ps[b] = po
-            for t in range(2):
-                for mm in range(2):
-                    s = 2 * t + mm
-                    rows = slice(P * s, P * s + P)
-                    nc.tensor.matmul_mx(
-                        out=po[:, 2 * mm + t, :],
-                        lhsT=a_codes[b][:, rows].bitcast(FP8X4),
-                        lhsT_scale=a_scales[b][:, rows],
-                        rhs=r_codes[b][:].bitcast(FP8X4),
-                        rhs_scale=r_scales[b][:],
-                        start=True,
-                        stop=True,
-                    )
+            for T in range(4):
+                rows = slice(P * T, P * T + P)
+                nc.tensor.matmul_mx(
+                    out=po[:, T, :],
+                    lhsT=a_codes[b][:, rows].bitcast(FP8X4),
+                    lhsT_scale=a_scales[b][:, rows],
+                    rhs=r_codes[b][:].bitcast(FP8X4),
+                    rhs_scale=r_scales[b][:],
+                    start=True,
+                    stop=True,
+                )
 
         def out_exit(b):
             if b % 2 == 0:

@@ -27,8 +27,8 @@ def tile_gcn_kernel(tc, regional_means, adj, out):
         cm_pool = ctx.enter_context(tc.tile_pool(name="cmp", bufs=3))
         r_pool = ctx.enter_context(tc.tile_pool(name="rp", bufs=13))
         rg_pool = ctx.enter_context(tc.tile_pool(name="rgp", bufs=3))
-        rc_pool = ctx.enter_context(tc.tile_pool(name="rcp", bufs=6))
-        g_pool = ctx.enter_context(tc.tile_pool(name="gp", bufs=4))
+        rc_pool = ctx.enter_context(tc.tile_pool(name="rcp", bufs=7))
+        g_pool = ctx.enter_context(tc.tile_pool(name="gp", bufs=3))
         c_pool = ctx.enter_context(tc.tile_pool(name="cp", bufs=4))
         o_pool = ctx.enter_context(tc.tile_pool(name="op", bufs=OUT_BUFS))
         pt_pool = ctx.enter_context(tc.psum_pool(name="ptp", bufs=6))
@@ -37,12 +37,15 @@ def tile_gcn_kernel(tc, regional_means, adj, out):
 
         ident = const.tile([P, P], F32, name="ident")
         make_identity(nc, ident[:])
-        keep = const.tile([P, 2, P, 2], BF16, name="keep")
-        nc.vector.memset(keep[:], 1.0)
-        for t in range(2):
-            nc.vector.tensor_scalar(
-                out=keep[:, t, :, t], in0=ident[:], scalar1=-1.0, scalar2=1.0, op0=MULT, op1=ADD
-            )
+        fold = const.tile([P, P // 2], F32, name="fold")
+        nc.vector.tensor_tensor(out=fold[:], in0=ident[:, 0 : P // 2], in1=ident[:, P // 2 : P], op=ADD)
+        keep = const.tile([P, 2, 2, P // 2, 2, 2], BF16, name="keep")
+        nc.vector.memset(keep[:].rearrange("p a t c a2 e -> p (a t c a2 e)"), 1.0)
+        for a in range(2):
+            for t in range(2):
+                nc.vector.tensor_scalar(
+                    out=keep[:, a, t, :, a, t], in0=fold[:], scalar1=-1.0, scalar2=1.0, op0=MULT, op1=ADD
+                )
 
         adj_sb = {}
         masked = {}
@@ -60,7 +63,10 @@ def tile_gcn_kernel(tc, regional_means, adj, out):
         def load_adj(g):
             t = adj_pool.tile([P, 2, 4 * N], BF16, name="adj_sb")
             adj_sb[g] = t
-            nc.sync.dma_start(out=t[:], in_=adj[2 * g : 2 * g + 2].rearrange("b (p T) j -> p b (T j)", T=4))
+            nc.sync.dma_start(
+                out=t[:].rearrange("p a x -> p (a x)"),
+                in_=adj[2 * g : 2 * g + 2].rearrange("b (c T) j -> (b c) (T j)", T=8),
+            )
 
         def load_r(g):
             t = r_pool.tile([P, 2, 4, F], BF16, name="r_raw")
@@ -92,34 +98,37 @@ def tile_gcn_kernel(tc, regional_means, adj, out):
             masked[g] = cm
             for s in range(2):
                 nc.vector.tensor_tensor(
-                    out=cm[:, :, s, :].rearrange("p b (n e) -> p b n e", e=2),
-                    in0=adj_sb[g][:, :, 2 * N * s : 2 * N * s + 2 * N].rearrange("p b (n w) -> p b n w", w=4)[
+                    out=cm[:, :, s, :].rearrange("p a (n e) -> p a n e", e=2),
+                    in0=adj_sb[g][:, :, 2 * N * s : 2 * N * s + 2 * N].rearrange("p a (n w) -> p a n w", w=4)[
                         :, :, :, 2 * s : 2 * s + 2
                     ],
-                    in1=keep[:].rearrange("p t q e -> p (t q) e").unsqueeze(1).to_broadcast([P, 2, 2 * P, 2]),
+                    in1=keep[:].rearrange("p a t c a2 e -> p a (t c a2) e"),
                     op=MULT,
                 )
 
-        def transposes(b):
-            words = adj_sb[b // 2][:, b % 2].bitcast(F32)
-            mwords = masked[b // 2][:, b % 2].rearrange("p s x -> p (s x)").bitcast(F32)
-            for h in range(2):
-                pt = pt_pool.tile([P, 2, 2, P], F32, name="pt")
-                banks[(b, h)] = pt
-                for t in range(2):
-                    c0 = 256 * (2 * h + t)
-                    nc.tensor.transpose(pt[:, 1 - h, t, :], words[:, c0 + 1 - h : c0 + 256 : 2], ident[:])
-                for t in range(2):
-                    c0 = 256 * h + 128 * t
-                    nc.tensor.transpose(pt[:, h, t, :], mwords[:, c0 : c0 + 128], ident[:])
+        def transposes(g, sd):
+            words = adj_sb[g][:].rearrange("p a x -> p (a x)").bitcast(F32)
+            mwords = masked[g][:].rearrange("p a s x -> p (a s x)").bitcast(F32)
+            for t in range(2):
+                pt = pt_pool.tile([P, 4, P], F32, name="pt")
+                banks[(g, 2 * sd + t)] = pt
+                for a in range(2):
+                    c0 = 256 * (4 * a + 2 * sd + t)
+                    nc.tensor.transpose(pt[:, 2 * a + 1 - sd, :], words[:, c0 + 1 - sd : c0 + 256 : 2], ident[:])
+                for a in range(2):
+                    c0 = 512 * a + 256 * sd + 128 * t
+                    nc.tensor.transpose(pt[:, 2 * a + sd, :], mwords[:, c0 : c0 + 128], ident[:])
 
-        def exits(b):
-            g = g_pool.tile([P, 4 * N], BF16, name="grouped", align_bytes=64)
-            grouped[b] = g
-            gw = g[:].bitcast(F32).rearrange("p (T m s) -> p T m s", T=4, s=2)
-            for h in range(2):
+        def exits(g, sd):
+            if sd == 0:
+                grouped[g] = g_pool.tile([P, 2, 4 * N], BF16, name="grouped", align_bytes=64)
+            gw = grouped[g][:].rearrange("p b x -> p (b x)").bitcast(F32).rearrange(
+                "p (b r c x) -> p b r c x", b=2, r=4, x=4
+            )
+            for t in range(2):
+                r = 2 * sd + t
                 nc.scalar.copy(
-                    out=gw[:, 2 * h : 2 * h + 2, :, :], in_=banks[(b, h)][:].rearrange("p s t m -> p t m s")
+                    out=gw[:, :, r, :, :], in_=banks[(g, r)][:].rearrange("q x (b c) -> q b c x", b=2)
                 )
 
         def quantise_a(b):
@@ -127,17 +136,17 @@ def tile_gcn_kernel(tc, regional_means, adj, out):
             sc = c_pool.tile([P, N], U8, name="a_scales", align_bytes=64)
             a_codes[b] = ac
             a_scales[b] = sc
-            nc.vector.quantize_mx(out=ac[:].bitcast(FP8X4), scales=sc[:], in_=grouped[b][:])
+            nc.vector.quantize_mx(out=ac[:].bitcast(FP8X4), scales=sc[:], in_=grouped[b // 2][:, b % 2, :])
 
         def multiply(b):
             po = po_pool.tile([P, 4, F], F32, name="po")
             o_ps[b] = po
-            for T in range(4):
-                rows = slice(P * T, P * T + P)
+            for r in range(4):
+                cols = slice(P * r, P * r + P)
                 nc.tensor.matmul_mx(
-                    out=po[:, T, :],
-                    lhsT=a_codes[b][:, rows].bitcast(FP8X4),
-                    lhsT_scale=a_scales[b][:, rows],
+                    out=po[:, r, :],
+                    lhsT=a_codes[b][:, cols].bitcast(FP8X4),
+                    lhsT_scale=a_scales[b][:, cols],
                     rhs=r_codes[b][:].bitcast(FP8X4),
                     rhs_scale=r_scales[b][:],
                     start=True,
@@ -151,8 +160,8 @@ def tile_gcn_kernel(tc, regional_means, adj, out):
 
         def store(g):
             nc.sync.dma_start(
-                out=out[2 * g : 2 * g + 2].rearrange("b (m T) f -> m b (T f)", T=4),
-                in_=o_sb[g][:].rearrange("m b T f -> m b (T f)"),
+                out=out[2 * g : 2 * g + 2].rearrange("b (m r) f -> m b (r f)", r=4),
+                in_=o_sb[g][:].rearrange("m b r f -> m b (r f)"),
             )
 
         loads = []
@@ -176,23 +185,23 @@ def tile_gcn_kernel(tc, regional_means, adj, out):
         regroup_r(0)
         regroup_r(1)
         quantise_r(0)
-        for i in range(B + 2):
+        for i in range(B + 3):
             if i % 2 == 1 and i + 1 < B:
                 mask((i + 1) // 2)
-            if 1 <= i <= B:
-                quantise_a(i - 1)
+            if 2 <= i < B + 2:
+                quantise_a(i - 2)
             if i + 2 < B:
                 regroup_r(i + 2)
             if i + 1 < B:
                 quantise_r(i + 1)
             if i < B:
-                transposes(i)
-            if i >= 2:
-                multiply(i - 2)
+                transposes(i // 2, i % 2)
+            if i >= 3:
+                multiply(i - 3)
             if i < B:
-                exits(i)
-            if i >= 2:
-                out_exit(i - 2)
-                if i % 2 == 1:
-                    store((i - 2) // 2)
+                exits(i // 2, i % 2)
+            if i >= 3:
+                out_exit(i - 3)
+                if i % 2 == 0:
+                    store((i - 3) // 2)
             issue_loads(i)

@@ -17,6 +17,7 @@ FLOPS = 2 * B * N * N * F
 STORE_LAG = 20
 ADJ_BUFS = STORE_LAG // 2 + 1
 OUT_BUFS = 13
+SPLIT_TILES = 4
 
 
 def tile_gcn_kernel(tc, regional_means, adj, out):
@@ -35,12 +36,12 @@ def tile_gcn_kernel(tc, regional_means, adj, out):
         po_pool = ctx.enter_context(tc.psum_pool(name="pop", bufs=2))
         ctx.enter_context(tc.manual_schedule())
 
+        keep = const.tile([P, 2, 2, P // 2, 2, 2], BF16, name="keep")
+        nc.vector.memset(keep[:].rearrange("p a t c a2 e -> p (a t c a2 e)"), 1.0)
         ident = const.tile([P, P], F32, name="ident")
         make_identity(nc, ident[:])
         fold = const.tile([P, P // 2], F32, name="fold")
         nc.vector.tensor_tensor(out=fold[:], in0=ident[:, 0 : P // 2], in1=ident[:, P // 2 : P], op=ADD)
-        keep = const.tile([P, 2, 2, P // 2, 2, 2], BF16, name="keep")
-        nc.vector.memset(keep[:].rearrange("p a t c a2 e -> p (a t c a2 e)"), 1.0)
         for a in range(2):
             for t in range(2):
                 nc.vector.tensor_scalar(
@@ -68,6 +69,14 @@ def tile_gcn_kernel(tc, regional_means, adj, out):
                 in_=adj[2 * g : 2 * g + 2].rearrange("b (c T) j -> (b c) (T j)", T=8),
             )
 
+        def load_adj_half(g, s):
+            if s == 0:
+                adj_sb[g] = adj_pool.tile([P, 2, 4 * N], BF16, name="adj_sb")
+            nc.sync.dma_start(
+                out=adj_sb[g][:, :, 2 * N * s : 2 * N * s + 2 * N],
+                in_=adj[2 * g : 2 * g + 2].rearrange("b (c a s x) j -> (b c) a s (x j)", a=2, s=2, x=2)[:, :, s, :],
+            )
+
         def load_r(g):
             t = r_pool.tile([P, 2, 4, F], BF16, name="r_raw")
             r_raw[g] = t
@@ -93,18 +102,17 @@ def tile_gcn_kernel(tc, regional_means, adj, out):
                 out=rc[:].bitcast(FP8X4), scales=rs[:], in_=r_grp[b][:].rearrange("q f v -> q (f v)")
             )
 
-        def mask(g):
-            cm = cm_pool.tile([P, 2, 2, N], BF16, name="masked")
-            masked[g] = cm
-            for s in range(2):
-                nc.vector.tensor_tensor(
-                    out=cm[:, :, s, :].rearrange("p a (n e) -> p a n e", e=2),
-                    in0=adj_sb[g][:, :, 2 * N * s : 2 * N * s + 2 * N].rearrange("p a (n w) -> p a n w", w=4)[
-                        :, :, :, 2 * s : 2 * s + 2
-                    ],
-                    in1=keep[:].rearrange("p a t c a2 e -> p a (t c a2) e"),
-                    op=MULT,
-                )
+        def mask(g, s):
+            if s == 0:
+                masked[g] = cm_pool.tile([P, 2, 2, N], BF16, name="masked")
+            nc.vector.tensor_tensor(
+                out=masked[g][:, :, s, :].rearrange("p a (n e) -> p a n e", e=2),
+                in0=adj_sb[g][:, :, 2 * N * s : 2 * N * s + 2 * N].rearrange("p a (n w) -> p a n w", w=4)[
+                    :, :, :, 2 * s : 2 * s + 2
+                ],
+                in1=keep[:].rearrange("p a t c a2 e -> p a (t c a2) e"),
+                op=MULT,
+            )
 
         def transposes(g, sd):
             words = adj_sb[g][:].rearrange("p a x -> p (a x)").bitcast(F32)
@@ -167,33 +175,33 @@ def tile_gcn_kernel(tc, regional_means, adj, out):
         loads = []
         for g in range(B // 2):
             tick = max(2 * g - STORE_LAG, -1)
-            loads.append(("a", g, tick))
-            if g == 0:
-                loads.append(("r", 0, tick))
-            if g + 1 < B // 2:
-                loads.append(("r", g + 1, tick))
+            if g < SPLIT_TILES:
+                loads.extend([("h0", g, tick), ("r", g, tick), ("h1", g, tick)])
+            else:
+                loads.extend([("a", g, tick), ("r", g, tick)])
 
         def issue_loads(now):
             for kind, idx, tick in loads:
                 if tick == now and kind == "a":
                     load_adj(idx)
+                if tick == now and kind == "h0":
+                    load_adj_half(idx, 0)
+                if tick == now and kind == "h1":
+                    load_adj_half(idx, 1)
                 if tick == now and kind == "r":
                     load_r(idx)
 
         issue_loads(-1)
-        mask(0)
-        regroup_r(0)
-        regroup_r(1)
-        quantise_r(0)
+        mask(0, 0)
         for i in range(B + 3):
-            if i % 2 == 1 and i + 1 < B:
-                mask((i + 1) // 2)
+            if i + 1 < B:
+                mask((i + 1) // 2, (i + 1) % 2)
             if 2 <= i < B + 2:
                 quantise_a(i - 2)
-            if i + 2 < B:
-                regroup_r(i + 2)
-            if i + 1 < B:
-                quantise_r(i + 1)
+            if i < B:
+                regroup_r(i)
+            if 1 <= i < B + 1:
+                quantise_r(i - 1)
             if i < B:
                 transposes(i // 2, i % 2)
             if i >= 3:

@@ -25,7 +25,7 @@ def tile_gcn_kernel(tc, regional_means, adj, out):
     with ExitStack() as ctx:
         const = ctx.enter_context(tc.tile_pool(name="const", bufs=1))
         adj_pool = ctx.enter_context(tc.tile_pool(name="adjp", bufs=ADJ_BUFS))
-        cm_pool = ctx.enter_context(tc.tile_pool(name="cmp", bufs=3))
+        cm_pool = ctx.enter_context(tc.tile_pool(name="cmp", bufs=5))
         r_pool = ctx.enter_context(tc.tile_pool(name="rp", bufs=13))
         rg_pool = ctx.enter_context(tc.tile_pool(name="rgp", bufs=3))
         rc_pool = ctx.enter_context(tc.tile_pool(name="rcp", bufs=7))
@@ -62,20 +62,23 @@ def tile_gcn_kernel(tc, regional_means, adj, out):
         o_sb = {}
 
         def load_adj(g):
-            t = adj_pool.tile([P, 2, 4 * N], BF16, name="adj_sb")
+            t = adj_pool.tile([P, 4, 2 * N], BF16, name="adj_sb")
             adj_sb[g] = t
             nc.sync.dma_start(
-                out=t[:].rearrange("p a x -> p (a x)"),
+                out=t[:].rearrange("p k x -> p (k x)"),
                 in_=adj[2 * g : 2 * g + 2].rearrange("b (c T) j -> (b c) (T j)", T=8),
             )
 
         def load_adj_half(g, s):
             if s == 0:
-                adj_sb[g] = adj_pool.tile([P, 2, 4 * N], BF16, name="adj_sb")
+                adj_sb[g] = adj_pool.tile([P, 4, 2 * N], BF16, name="adj_sb")
             nc.sync.dma_start(
-                out=adj_sb[g][:, :, 2 * N * s : 2 * N * s + 2 * N],
+                out=adj_sb[g][:, 2 * s : 2 * s + 2, :],
                 in_=adj[2 * g : 2 * g + 2].rearrange("b (c a s x) j -> (b c) a s (x j)", a=2, s=2, x=2)[:, :, s, :],
             )
+
+        def blocks(g, s):
+            return (2 * s, 1) if g < SPLIT_TILES else (s, 2)
 
         def load_r(g):
             t = r_pool.tile([P, 2, 4, F], BF16, name="r_raw")
@@ -103,11 +106,11 @@ def tile_gcn_kernel(tc, regional_means, adj, out):
             )
 
         def mask(g, s):
-            if s == 0:
-                masked[g] = cm_pool.tile([P, 2, 2, N], BF16, name="masked")
+            k0, step = blocks(g, s)
+            masked[(g, s)] = cm_pool.tile([P, 2, N], BF16, name="masked")
             nc.vector.tensor_tensor(
-                out=masked[g][:, :, s, :].rearrange("p a (n e) -> p a n e", e=2),
-                in0=adj_sb[g][:, :, 2 * N * s : 2 * N * s + 2 * N].rearrange("p a (n w) -> p a n w", w=4)[
+                out=masked[(g, s)][:].rearrange("p a (n e) -> p a n e", e=2),
+                in0=adj_sb[g][:, k0 : k0 + step + 1 : step, :].rearrange("p a (n w) -> p a n w", w=4)[
                     :, :, :, 2 * s : 2 * s + 2
                 ],
                 in1=keep[:].rearrange("p a t c a2 e -> p a (t c a2) e"),
@@ -115,16 +118,17 @@ def tile_gcn_kernel(tc, regional_means, adj, out):
             )
 
         def transposes(g, sd):
-            words = adj_sb[g][:].rearrange("p a x -> p (a x)").bitcast(F32)
-            mwords = masked[g][:].rearrange("p a s x -> p (a s x)").bitcast(F32)
+            k0, step = blocks(g, sd)
+            words = adj_sb[g][:].rearrange("p k x -> p (k x)").bitcast(F32)
+            mwords = masked[(g, sd)][:].rearrange("p a x -> p (a x)").bitcast(F32)
             for t in range(2):
                 pt = pt_pool.tile([P, 4, P], F32, name="pt")
                 banks[(g, 2 * sd + t)] = pt
                 for a in range(2):
-                    c0 = 256 * (4 * a + 2 * sd + t)
+                    c0 = 512 * (k0 + step * a) + 256 * t
                     nc.tensor.transpose(pt[:, 2 * a + 1 - sd, :], words[:, c0 + 1 - sd : c0 + 256 : 2], ident[:])
                 for a in range(2):
-                    c0 = 512 * a + 256 * sd + 128 * t
+                    c0 = 256 * a + 128 * t
                     nc.tensor.transpose(pt[:, 2 * a + sd, :], mwords[:, c0 : c0 + 128], ident[:])
 
         def exits(g, sd):

@@ -17,7 +17,7 @@ FLOPS = 2 * B * N * N * F
 STORE_LAG = 20
 ADJ_BUFS = STORE_LAG // 2 + 1
 OUT_BUFS = 13
-SPLIT_TILES = 4
+SPLIT_TILES = 0
 
 
 def tile_gcn_kernel(tc, regional_means, adj, out):
@@ -29,9 +29,10 @@ def tile_gcn_kernel(tc, regional_means, adj, out):
         r_pool = ctx.enter_context(tc.tile_pool(name="rp", bufs=13))
         rg_pool = ctx.enter_context(tc.tile_pool(name="rgp", bufs=3))
         rc_pool = ctx.enter_context(tc.tile_pool(name="rcp", bufs=7))
-        g_pool = ctx.enter_context(tc.tile_pool(name="gp", bufs=3))
+        g_pool = ctx.enter_context(tc.tile_pool(name="gp", bufs=4))
         c_pool = ctx.enter_context(tc.tile_pool(name="cp", bufs=4))
         o_pool = ctx.enter_context(tc.tile_pool(name="op", bufs=OUT_BUFS))
+        oh_pool = ctx.enter_context(tc.tile_pool(name="ohp", bufs=2))
         pt_pool = ctx.enter_context(tc.psum_pool(name="ptp", bufs=6))
         po_pool = ctx.enter_context(tc.psum_pool(name="pop", bufs=2))
         ctx.enter_context(tc.manual_schedule())
@@ -131,49 +132,61 @@ def tile_gcn_kernel(tc, regional_means, adj, out):
                     c0 = 256 * a + 128 * t
                     nc.tensor.transpose(pt[:, 2 * a + sd, :], mwords[:, c0 : c0 + 128], ident[:])
 
-        def exits(g, sd):
-            if sd == 0:
-                grouped[g] = g_pool.tile([P, 2, 4 * N], BF16, name="grouped", align_bytes=64)
-            gw = grouped[g][:].rearrange("p b x -> p (b x)").bitcast(F32).rearrange(
-                "p (b r c x) -> p b r c x", b=2, r=4, x=4
-            )
+        def exits(i):
+            g, sd = i // 2, i % 2
+            grouped[i] = g_pool.tile([P, 4 * N], BF16, name="grouped", align_bytes=64)
+            gw = grouped[i][:].bitcast(F32).rearrange("p (t b c x) -> p t b c x", t=2, b=2, x=4)
             for t in range(2):
-                r = 2 * sd + t
                 nc.scalar.copy(
-                    out=gw[:, :, r, :, :], in_=banks[(g, r)][:].rearrange("q x (b c) -> q b c x", b=2)
+                    out=gw[:, t, :, :, :], in_=banks[(g, 2 * sd + t)][:].rearrange("q x (b c) -> q b c x", b=2)
                 )
 
-        def quantise_a(b):
+        def quantise_a(i):
             ac = c_pool.tile([P, N], U32, name="a_codes", align_bytes=64)
             sc = c_pool.tile([P, N], U8, name="a_scales", align_bytes=64)
-            a_codes[b] = ac
-            a_scales[b] = sc
-            nc.vector.quantize_mx(out=ac[:].bitcast(FP8X4), scales=sc[:], in_=grouped[b // 2][:, b % 2, :])
+            a_codes[i] = ac
+            a_scales[i] = sc
+            nc.vector.quantize_mx(out=ac[:].bitcast(FP8X4), scales=sc[:], in_=grouped[i][:])
 
-        def multiply(b):
+        def multiply(i):
             po = po_pool.tile([P, 4, F], F32, name="po")
-            o_ps[b] = po
-            for r in range(4):
-                cols = slice(P * r, P * r + P)
+            o_ps[i] = po
+            for k in range(4):
+                b = 2 * (i // 2) + k % 2
+                cols = slice(P * k, P * k + P)
                 nc.tensor.matmul_mx(
-                    out=po[:, r, :],
-                    lhsT=a_codes[b][:, cols].bitcast(FP8X4),
-                    lhsT_scale=a_scales[b][:, cols],
+                    out=po[:, k, :],
+                    lhsT=a_codes[i][:, cols].bitcast(FP8X4),
+                    lhsT_scale=a_scales[i][:, cols],
                     rhs=r_codes[b][:].bitcast(FP8X4),
                     rhs_scale=r_scales[b][:],
                     start=True,
                     stop=True,
                 )
 
-        def out_exit(b):
-            if b % 2 == 0:
-                o_sb[b // 2] = o_pool.tile([P, 2, 4, F], F32, name="o_sb")
-            nc.scalar.copy(out=o_sb[b // 2][:, b % 2], in_=o_ps[b][:])
+        def out_exit(i):
+            g, sd = i // 2, i % 2
+            if sd == 0:
+                o_sb[g] = o_pool.tile([P, 2, 4, F], F32, name="o_sb")
+            nc.scalar.copy(
+                out=o_sb[g][:, :, 2 * sd : 2 * sd + 2, :], in_=o_ps[i][:].rearrange("m (t b) f -> m b t f", b=2)
+            )
 
         def store(g):
             nc.sync.dma_start(
                 out=out[2 * g : 2 * g + 2].rearrange("b (m r) f -> m b (r f)", r=4),
                 in_=o_sb[g][:].rearrange("m b r f -> m b (r f)"),
+            )
+
+        def last_exit_and_store(i):
+            g, sd = i // 2, i % 2
+            oh = oh_pool.tile([P, 2, 2, F], F32, name="o_half")
+            nc.scalar.copy(out=oh[:], in_=o_ps[i][:].rearrange("m (t b) f -> m b t f", b=2))
+            nc.sync.dma_start(
+                out=out[2 * g : 2 * g + 2].rearrange("b (m r) f -> m b (r f)", r=4)[
+                    :, :, 2 * F * sd : 2 * F * sd + 2 * F
+                ],
+                in_=oh[:].rearrange("m b t f -> m b (t f)"),
             )
 
         loads = []
@@ -197,23 +210,26 @@ def tile_gcn_kernel(tc, regional_means, adj, out):
 
         issue_loads(-1)
         mask(0, 0)
-        for i in range(B + 3):
+        regroup_r(0)
+        for i in range(B + 2):
             if i + 1 < B:
                 mask((i + 1) // 2, (i + 1) % 2)
-            if 2 <= i < B + 2:
-                quantise_a(i - 2)
-            if i < B:
-                regroup_r(i)
             if 1 <= i < B + 1:
-                quantise_r(i - 1)
+                quantise_a(i - 1)
+            if i + 1 < B:
+                regroup_r(i + 1)
+            if i < B:
+                quantise_r(i)
             if i < B:
                 transposes(i // 2, i % 2)
-            if i >= 3:
-                multiply(i - 3)
+            if i >= 2:
+                multiply(i - 2)
             if i < B:
-                exits(i // 2, i % 2)
-            if i >= 3:
-                out_exit(i - 3)
-                if i % 2 == 0:
-                    store((i - 3) // 2)
+                exits(i)
+            if 2 <= i < B:
+                out_exit(i - 2)
+                if i % 2 == 1:
+                    store((i - 2) // 2)
+            if i >= B:
+                last_exit_and_store(i - 2)
             issue_loads(i)

@@ -14,40 +14,61 @@ ADD = mybir.AluOpType.add
 B, N, F, P = 32, 512, 128, 128
 FLOPS = 2 * B * N * N * F
 
-STORE_LAG = 20
-ADJ_BUFS = STORE_LAG // 2 + 1
-OUT_BUFS = 13
-SPLIT_TILES = 0
+SIZES = (2, 2, 2, 2, 2, 4, 4, 4, 4, 4, 2)
+ADJ_BUFS = {2: 3, 4: 4}
+OUT_BUFS = {2: 6, 4: 5}
+RB = 4
+R_BUFS = 6
 
 
 def tile_gcn_kernel(tc, regional_means, adj, out):
     nc = tc.nc
     with ExitStack() as ctx:
         const = ctx.enter_context(tc.tile_pool(name="const", bufs=1))
-        adj_pool = ctx.enter_context(tc.tile_pool(name="adjp", bufs=ADJ_BUFS))
-        cm_pool = ctx.enter_context(tc.tile_pool(name="cmp", bufs=5))
-        r_pool = ctx.enter_context(tc.tile_pool(name="rp", bufs=13))
+        adj_pools = {
+            2: ctx.enter_context(tc.tile_pool(name="adj2", bufs=ADJ_BUFS[2])),
+            4: ctx.enter_context(tc.tile_pool(name="adj4", bufs=ADJ_BUFS[4])),
+        }
+        o_pools = {
+            2: ctx.enter_context(tc.tile_pool(name="o2", bufs=OUT_BUFS[2])),
+            4: ctx.enter_context(tc.tile_pool(name="o4", bufs=OUT_BUFS[4])),
+        }
+        cm_pool = ctx.enter_context(tc.tile_pool(name="cmp", bufs=4))
+        r_pool = ctx.enter_context(tc.tile_pool(name="rp", bufs=R_BUFS))
         rg_pool = ctx.enter_context(tc.tile_pool(name="rgp", bufs=3))
-        rc_pool = ctx.enter_context(tc.tile_pool(name="rcp", bufs=7))
+        rc_pool = ctx.enter_context(tc.tile_pool(name="rcp", bufs=10))
         g_pool = ctx.enter_context(tc.tile_pool(name="gp", bufs=4))
         c_pool = ctx.enter_context(tc.tile_pool(name="cp", bufs=4))
-        o_pool = ctx.enter_context(tc.tile_pool(name="op", bufs=OUT_BUFS))
-        oh_pool = ctx.enter_context(tc.tile_pool(name="ohp", bufs=2))
         pt_pool = ctx.enter_context(tc.psum_pool(name="ptp", bufs=6))
         po_pool = ctx.enter_context(tc.psum_pool(name="pop", bufs=2))
         ctx.enter_context(tc.manual_schedule())
 
-        keep = const.tile([P, 2, 2, P // 2, 2, 2], BF16, name="keep")
-        nc.vector.memset(keep[:].rearrange("p a t c a2 e -> p (a t c a2 e)"), 1.0)
+        keep2 = const.tile([P, 2, 2, P // 2, 2, 2], BF16, name="keep2")
+        nc.vector.memset(keep2[:].rearrange("p a t c a2 e -> p (a t c a2 e)"), 1.0)
         ident = const.tile([P, P], F32, name="ident")
         make_identity(nc, ident[:])
-        fold = const.tile([P, P // 2], F32, name="fold")
-        nc.vector.tensor_tensor(out=fold[:], in0=ident[:, 0 : P // 2], in1=ident[:, P // 2 : P], op=ADD)
+        keep4 = const.tile([P, 2, 4, P // 4, 4, 2], BF16, name="keep4")
+        nc.gpsimd.memset(keep4[:].rearrange("p s a c a2 e -> p (s a c a2 e)"), 1.0)
+        fold64 = const.tile([P, P // 2], F32, name="fold64")
+        nc.vector.tensor_tensor(out=fold64[:], in0=ident[:, 0 : P // 2], in1=ident[:, P // 2 : P], op=ADD)
         for a in range(2):
             for t in range(2):
                 nc.vector.tensor_scalar(
-                    out=keep[:, a, t, :, a, t], in0=fold[:], scalar1=-1.0, scalar2=1.0, op0=MULT, op1=ADD
+                    out=keep2[:, a, t, :, a, t], in0=fold64[:], scalar1=-1.0, scalar2=1.0, op0=MULT, op1=ADD
                 )
+        fold32 = const.tile([P, P // 4], F32, name="fold32")
+        nc.gpsimd.tensor_tensor(out=fold32[:], in0=fold64[:, 0 : P // 4], in1=fold64[:, P // 4 : P // 2], op=ADD)
+        for s in range(2):
+            for a in range(4):
+                nc.gpsimd.tensor_scalar(
+                    out=keep4[:, s, a, :, a, s], in0=fold32[:], scalar1=-1.0, scalar2=1.0, op0=MULT, op1=ADD
+                )
+
+        tiles = []
+        ticks = []
+        for size in SIZES:
+            tiles.append((len(ticks), size))
+            ticks.extend([(len(tiles) - 1, tau) for tau in range(size)])
 
         adj_sb = {}
         masked = {}
@@ -62,31 +83,21 @@ def tile_gcn_kernel(tc, regional_means, adj, out):
         o_ps = {}
         o_sb = {}
 
-        def load_adj(g):
-            t = adj_pool.tile([P, 4, 2 * N], BF16, name="adj_sb")
-            adj_sb[g] = t
+        def load_adj(z):
+            b0, size = tiles[z]
+            t = adj_pools[size].tile([P, size, 4 * N], BF16, name="adj_sb")
+            adj_sb[z] = t
             nc.sync.dma_start(
-                out=t[:].rearrange("p k x -> p (k x)"),
-                in_=adj[2 * g : 2 * g + 2].rearrange("b (c T) j -> (b c) (T j)", T=8),
+                out=t[:].rearrange("p a x -> p (a x)"),
+                in_=adj[b0 : b0 + size].rearrange("b (c T) j -> (b c) (T j)", T=4 * size),
             )
 
-        def load_adj_half(g, s):
-            if s == 0:
-                adj_sb[g] = adj_pool.tile([P, 4, 2 * N], BF16, name="adj_sb")
-            nc.sync.dma_start(
-                out=adj_sb[g][:, 2 * s : 2 * s + 2, :],
-                in_=adj[2 * g : 2 * g + 2].rearrange("b (c a s x) j -> (b c) a s (x j)", a=2, s=2, x=2)[:, :, s, :],
-            )
-
-        def blocks(g, s):
-            return (2 * s, 1) if g < SPLIT_TILES else (s, 2)
-
-        def load_r(g):
-            t = r_pool.tile([P, 2, 4, F], BF16, name="r_raw")
-            r_raw[g] = t
+        def load_r(k):
+            t = r_pool.tile([P, RB, 4, F], BF16, name="r_raw")
+            r_raw[k] = t
             nc.sync.dma_start(
                 out=t[:].rearrange("q b v f -> q b (v f)"),
-                in_=regional_means[2 * g : 2 * g + 2].rearrange("b (q v) f -> q b (v f)", v=4),
+                in_=regional_means[RB * k : RB * k + RB].rearrange("b (q v) f -> q b (v f)", v=4),
             )
 
         def regroup_r(b):
@@ -94,7 +105,7 @@ def tile_gcn_kernel(tc, regional_means, adj, out):
             r_grp[b] = rg
             nc.vector.tensor_copy(
                 out=rg[:].rearrange("q (c i) v -> q c v i", i=4),
-                in_=r_raw[b // 2][:, b % 2].rearrange("q v (c i) -> q c v i", i=4),
+                in_=r_raw[b // RB][:, b % RB].rearrange("q v (c i) -> q c v i", i=4),
             )
 
         def quantise_r(b):
@@ -106,40 +117,52 @@ def tile_gcn_kernel(tc, regional_means, adj, out):
                 out=rc[:].bitcast(FP8X4), scales=rs[:], in_=r_grp[b][:].rearrange("q f v -> q (f v)")
             )
 
-        def mask(g, s):
-            k0, step = blocks(g, s)
-            masked[(g, s)] = cm_pool.tile([P, 2, N], BF16, name="masked")
+        def mask(i):
+            z, tau = ticks[i]
+            size = tiles[z][1]
+            nr = 4 // size
+            u = nr * tau // 2
+            cm = cm_pool.tile([P, size, 2 * P * nr], BF16, name="masked")
+            masked[i] = cm
+            if size == 2:
+                keep = keep2[:].rearrange("p a t c a2 e -> p a (t c a2) e")
+            else:
+                keep = keep4[:, tau % 2].rearrange("p a c a2 e -> p a (c a2) e")
             nc.vector.tensor_tensor(
-                out=masked[(g, s)][:].rearrange("p a (n e) -> p a n e", e=2),
-                in0=adj_sb[g][:, k0 : k0 + step + 1 : step, :].rearrange("p a (n w) -> p a n w", w=4)[
-                    :, :, :, 2 * s : 2 * s + 2
+                out=cm[:].rearrange("p a (n e) -> p a n e", e=2),
+                in0=adj_sb[z][:, :, nr * N * tau : nr * N * (tau + 1)].rearrange("p a (n w) -> p a n w", w=4)[
+                    :, :, :, 2 * u : 2 * u + 2
                 ],
-                in1=keep[:].rearrange("p a t c a2 e -> p a (t c a2) e"),
+                in1=keep,
                 op=MULT,
             )
 
-        def transposes(g, sd):
-            k0, step = blocks(g, sd)
-            words = adj_sb[g][:].rearrange("p k x -> p (k x)").bitcast(F32)
-            mwords = masked[(g, sd)][:].rearrange("p a x -> p (a x)").bitcast(F32)
-            for t in range(2):
+        def transposes(i):
+            z, tau = ticks[i]
+            size = tiles[z][1]
+            nr = 4 // size
+            u = nr * tau // 2
+            words = adj_sb[z][:].rearrange("p a x -> p (a x)").bitcast(F32)
+            mwords = masked[i][:].rearrange("p a x -> p (a x)").bitcast(F32)
+            for j in range(2):
                 pt = pt_pool.tile([P, 4, P], F32, name="pt")
-                banks[(g, 2 * sd + t)] = pt
-                for a in range(2):
-                    c0 = 512 * (k0 + step * a) + 256 * t
-                    nc.tensor.transpose(pt[:, 2 * a + 1 - sd, :], words[:, c0 + 1 - sd : c0 + 256 : 2], ident[:])
-                for a in range(2):
-                    c0 = 256 * a + 128 * t
-                    nc.tensor.transpose(pt[:, 2 * a + sd, :], mwords[:, c0 : c0 + 128], ident[:])
+                banks[(i, j)] = pt
+                rows = [(a2, j) if size == 2 else (2 * j + a2, 0) for a2 in range(2)]
+                for a2, (a, t) in enumerate(rows):
+                    c0 = 256 * (4 * a + nr * tau + t)
+                    nc.tensor.transpose(pt[:, 2 * a2 + 1 - u, :], words[:, c0 + 1 - u : c0 + 256 : 2], ident[:])
+                for a2, (a, t) in enumerate(rows):
+                    c0 = 128 * (nr * a + t)
+                    nc.tensor.transpose(pt[:, 2 * a2 + u, :], mwords[:, c0 : c0 + 128], ident[:])
 
         def exits(i):
-            g, sd = i // 2, i % 2
-            grouped[i] = g_pool.tile([P, 4 * N], BF16, name="grouped", align_bytes=64)
-            gw = grouped[i][:].bitcast(F32).rearrange("p (t b c x) -> p t b c x", t=2, b=2, x=4)
-            for t in range(2):
-                nc.scalar.copy(
-                    out=gw[:, t, :, :, :], in_=banks[(g, 2 * sd + t)][:].rearrange("q x (b c) -> q b c x", b=2)
-                )
+            size = tiles[ticks[i][0]][1]
+            gt = g_pool.tile([P, 4 * N], BF16, name="grouped", align_bytes=64)
+            grouped[i] = gt
+            gw = gt[:].bitcast(F32).rearrange("p (t n k x) -> p t n k x", t=4 // size, k=size // 2, x=4)
+            for j in range(2):
+                t, k = (j, 0) if size == 2 else (0, j)
+                nc.scalar.copy(out=gw[:, t, :, k, :], in_=banks[(i, j)][:].rearrange("q x n -> q n x"))
 
         def quantise_a(i):
             ac = c_pool.tile([P, N], U32, name="a_codes", align_bytes=64)
@@ -149,10 +172,11 @@ def tile_gcn_kernel(tc, regional_means, adj, out):
             nc.vector.quantize_mx(out=ac[:].bitcast(FP8X4), scales=sc[:], in_=grouped[i][:])
 
         def multiply(i):
+            b0, size = tiles[ticks[i][0]]
             po = po_pool.tile([P, 4, F], F32, name="po")
             o_ps[i] = po
             for k in range(4):
-                b = 2 * (i // 2) + k % 2
+                b = b0 + k % size
                 cols = slice(P * k, P * k + P)
                 nc.tensor.matmul_mx(
                     out=po[:, k, :],
@@ -165,71 +189,73 @@ def tile_gcn_kernel(tc, regional_means, adj, out):
                 )
 
         def out_exit(i):
-            g, sd = i // 2, i % 2
-            if sd == 0:
-                o_sb[g] = o_pool.tile([P, 2, 4, F], F32, name="o_sb")
+            z, tau = ticks[i]
+            size = tiles[z][1]
+            nr = 4 // size
+            if tau == 0:
+                o_sb[z] = o_pools[size].tile([P, size, 4, F], F32, name="o_sb")
             nc.scalar.copy(
-                out=o_sb[g][:, :, 2 * sd : 2 * sd + 2, :], in_=o_ps[i][:].rearrange("m (t b) f -> m b t f", b=2)
+                out=o_sb[z][:, :, nr * tau : nr * tau + nr, :],
+                in_=o_ps[i][:].rearrange("m (t b) f -> m b t f", t=nr),
             )
 
-        def store(g):
+        def store(z):
+            b0, size = tiles[z]
             nc.sync.dma_start(
-                out=out[2 * g : 2 * g + 2].rearrange("b (m r) f -> m b (r f)", r=4),
-                in_=o_sb[g][:].rearrange("m b r f -> m b (r f)"),
+                out=out[b0 : b0 + size].rearrange("b (m r) f -> m b (r f)", r=4),
+                in_=o_sb[z][:].rearrange("m b r f -> m b (r f)"),
             )
 
-        def last_exit_and_store(i):
-            g, sd = i // 2, i % 2
-            oh = oh_pool.tile([P, 2, 2, F], F32, name="o_half")
-            nc.scalar.copy(out=oh[:], in_=o_ps[i][:].rearrange("m (t b) f -> m b t f", b=2))
-            nc.sync.dma_start(
-                out=out[2 * g : 2 * g + 2].rearrange("b (m r) f -> m b (r f)", r=4)[
-                    :, :, 2 * F * sd : 2 * F * sd + 2 * F
-                ],
-                in_=oh[:].rearrange("m b t f -> m b (t f)"),
-            )
-
+        needs = [(max(b0 - 1, -1), 0, z) for z, (b0, size) in enumerate(tiles)]
+        needs.extend([(max(RB * k - 3, -1), 1, k) for k in range(B // RB)])
         loads = []
-        for g in range(B // 2):
-            tick = max(2 * g - STORE_LAG, -1)
-            if g < SPLIT_TILES:
-                loads.extend([("h0", g, tick), ("r", g, tick), ("h1", g, tick)])
-            else:
-                loads.extend([("a", g, tick), ("r", g, tick)])
+        seen = {2: [], 4: []}
+        tick = -1
+        for need, kind, idx in sorted(needs):
+            if kind == 0:
+                b0, size = tiles[idx]
+                if len(seen[size]) >= ADJ_BUFS[size]:
+                    old_b0, old_size = tiles[seen[size][len(seen[size]) - ADJ_BUFS[size]]]
+                    tick = max(tick, old_b0 + old_size - 1)
+                seen[size].append(idx)
+            elif idx >= R_BUFS:
+                tick = max(tick, RB * (idx - R_BUFS))
+            loads.append((kind, idx, tick))
+        last_load_tick = tick
 
         def issue_loads(now):
-            for kind, idx, tick in loads:
-                if tick == now and kind == "a":
+            for kind, idx, when in loads:
+                if when == now and kind == 0:
                     load_adj(idx)
-                if tick == now and kind == "h0":
-                    load_adj_half(idx, 0)
-                if tick == now and kind == "h1":
-                    load_adj_half(idx, 1)
-                if tick == now and kind == "r":
+                if when == now and kind == 1:
                     load_r(idx)
 
         issue_loads(-1)
-        mask(0, 0)
-        regroup_r(0)
+        mask(0)
         for i in range(B + 2):
             if i + 1 < B:
-                mask((i + 1) // 2, (i + 1) % 2)
+                mask(i + 1)
             if 1 <= i < B + 1:
                 quantise_a(i - 1)
-            if i + 1 < B:
-                regroup_r(i + 1)
+            if i == 0:
+                regroup_r(0)
+                regroup_r(1)
+                quantise_r(0)
+                regroup_r(2)
+                quantise_r(1)
+            if i + 3 < B:
+                regroup_r(i + 3)
+            if i + 2 < B:
+                quantise_r(i + 2)
             if i < B:
-                quantise_r(i)
-            if i < B:
-                transposes(i // 2, i % 2)
+                transposes(i)
             if i >= 2:
                 multiply(i - 2)
             if i < B:
                 exits(i)
-            if 2 <= i < B:
+            if i >= 2:
                 out_exit(i - 2)
-                if i % 2 == 1:
-                    store((i - 2) // 2)
-            if i >= B:
-                last_exit_and_store(i - 2)
             issue_loads(i)
+            for z, (b0, size) in enumerate(tiles):
+                if max(b0 + size + 1, last_load_tick) == i:
+                    store(z)

@@ -14,9 +14,9 @@ ADD = mybir.AluOpType.add
 B, N, F, P = 32, 512, 128, 128
 FLOPS = 2 * B * N * N * F
 
-SIZES = (2, 2, 2, 2, 2, 4, 4, 4, 4, 4, 2)
-ADJ_BUFS = {2: 3, 4: 4}
-OUT_BUFS = {2: 6, 4: 5}
+SIZES = (2, 2, 2, 2, 2, 2, 2, 2, 2, 2, 2, 2, 2, 2, 2, 2)
+ADJ_BUFS = {2: 9, 4: 4}
+OUT_BUFS = {2: 16, 4: 5}
 RB = 4
 R_BUFS = 6
 

from contextlib import ExitStack

import concourse.mybir as mybir
from concourse.masks import make_identity

FP8X4 = mybir.dt.float8_e4m3fn_x4
BF16 = mybir.dt.bfloat16
F32 = mybir.dt.float32
U32 = mybir.dt.uint32
U8 = mybir.dt.uint8
MULT = mybir.AluOpType.mult
ADD = mybir.AluOpType.add

B, N, F, P = 32, 512, 128, 128
FLOPS = 2 * B * N * N * F

SIZES = (2, 2, 2, 2, 2, 2, 2, 2, 2, 2, 2, 2, 2, 2, 2, 2)
ADJ_BUFS = {2: 9, 4: 4}
OUT_BUFS = {2: 16, 4: 5}
RB = 4
R_BUFS = 6


def tile_gcn_kernel(tc, regional_means, adj, out):
    nc = tc.nc
    with ExitStack() as ctx:
        const = ctx.enter_context(tc.tile_pool(name="const", bufs=1))
        adj_pools = {
            2: ctx.enter_context(tc.tile_pool(name="adj2", bufs=ADJ_BUFS[2])),
            4: ctx.enter_context(tc.tile_pool(name="adj4", bufs=ADJ_BUFS[4])),
        }
        o_pools = {
            2: ctx.enter_context(tc.tile_pool(name="o2", bufs=OUT_BUFS[2])),
            4: ctx.enter_context(tc.tile_pool(name="o4", bufs=OUT_BUFS[4])),
        }
        cm_pool = ctx.enter_context(tc.tile_pool(name="cmp", bufs=4))
        r_pool = ctx.enter_context(tc.tile_pool(name="rp", bufs=R_BUFS))
        rg_pool = ctx.enter_context(tc.tile_pool(name="rgp", bufs=3))
        rc_pool = ctx.enter_context(tc.tile_pool(name="rcp", bufs=10))
        g_pool = ctx.enter_context(tc.tile_pool(name="gp", bufs=4))
        c_pool = ctx.enter_context(tc.tile_pool(name="cp", bufs=4))
        pt_pool = ctx.enter_context(tc.psum_pool(name="ptp", bufs=6))
        po_pool = ctx.enter_context(tc.psum_pool(name="pop", bufs=2))
        ctx.enter_context(tc.manual_schedule())

        keep2 = const.tile([P, 2, 2, P // 2, 2, 2], BF16, name="keep2")
        nc.vector.memset(keep2[:].rearrange("p a t c a2 e -> p (a t c a2 e)"), 1.0)
        ident = const.tile([P, P], F32, name="ident")
        make_identity(nc, ident[:])
        keep4 = const.tile([P, 2, 4, P // 4, 4, 2], BF16, name="keep4")
        nc.gpsimd.memset(keep4[:].rearrange("p s a c a2 e -> p (s a c a2 e)"), 1.0)
        fold64 = const.tile([P, P // 2], F32, name="fold64")
        nc.vector.tensor_tensor(out=fold64[:], in0=ident[:, 0 : P // 2], in1=ident[:, P // 2 : P], op=ADD)
        for a in range(2):
            for t in range(2):
                nc.vector.tensor_scalar(
                    out=keep2[:, a, t, :, a, t], in0=fold64[:], scalar1=-1.0, scalar2=1.0, op0=MULT, op1=ADD
                )
        fold32 = const.tile([P, P // 4], F32, name="fold32")
        nc.gpsimd.tensor_tensor(out=fold32[:], in0=fold64[:, 0 : P // 4], in1=fold64[:, P // 4 : P // 2], op=ADD)
        for s in range(2):
            for a in range(4):
                nc.gpsimd.tensor_scalar(
                    out=keep4[:, s, a, :, a, s], in0=fold32[:], scalar1=-1.0, scalar2=1.0, op0=MULT, op1=ADD
                )

        tiles = []
        ticks = []
        for size in SIZES:
            tiles.append((len(ticks), size))
            ticks.extend([(len(tiles) - 1, tau) for tau in range(size)])

        adj_sb = {}
        masked = {}
        r_raw = {}
        r_grp = {}
        r_codes = {}
        r_scales = {}
        banks = {}
        grouped = {}
        a_codes = {}
        a_scales = {}
        o_ps = {}
        o_sb = {}

        def load_adj(z):
            b0, size = tiles[z]
            t = adj_pools[size].tile([P, size, 4 * N], BF16, name="adj_sb")
            adj_sb[z] = t
            nc.sync.dma_start(
                out=t[:].rearrange("p a x -> p (a x)"),
                in_=adj[b0 : b0 + size].rearrange("b (c T) j -> (b c) (T j)", T=4 * size),
            )

        def load_r(k):
            t = r_pool.tile([P, RB, 4, F], BF16, name="r_raw")
            r_raw[k] = t
            nc.sync.dma_start(
                out=t[:].rearrange("q b v f -> q b (v f)"),
                in_=regional_means[RB * k : RB * k + RB].rearrange("b (q v) f -> q b (v f)", v=4),
            )

        def regroup_r(b):
            rg = rg_pool.tile([P, F, 4], BF16, name="r_grp", align_bytes=64)
            r_grp[b] = rg
            nc.vector.tensor_copy(
                out=rg[:].rearrange("q (c i) v -> q c v i", i=4),
                in_=r_raw[b // RB][:, b % RB].rearrange("q v (c i) -> q c v i", i=4),
            )

        def quantise_r(b):
            rc = rc_pool.tile([P, F], U32, name="r_codes", align_bytes=64)
            rs = rc_pool.tile([P, F], U8, name="r_scales", align_bytes=64)
            r_codes[b] = rc
            r_scales[b] = rs
            nc.vector.quantize_mx(
                out=rc[:].bitcast(FP8X4), scales=rs[:], in_=r_grp[b][:].rearrange("q f v -> q (f v)")
            )

        def mask(i):
            z, tau = ticks[i]
            size = tiles[z][1]
            nr = 4 // size
            u = nr * tau // 2
            cm = cm_pool.tile([P, size, 2 * P * nr], BF16, name="masked")
            masked[i] = cm
            if size == 2:
                keep = keep2[:].rearrange("p a t c a2 e -> p a (t c a2) e")
            else:
                keep = keep4[:, tau % 2].rearrange("p a c a2 e -> p a (c a2) e")
            nc.vector.tensor_tensor(
                out=cm[:].rearrange("p a (n e) -> p a n e", e=2),
                in0=adj_sb[z][:, :, nr * N * tau : nr * N * (tau + 1)].rearrange("p a (n w) -> p a n w", w=4)[
                    :, :, :, 2 * u : 2 * u + 2
                ],
                in1=keep,
                op=MULT,
            )

        def transposes(i):
            z, tau = ticks[i]
            size = tiles[z][1]
            nr = 4 // size
            u = nr * tau // 2
            words = adj_sb[z][:].rearrange("p a x -> p (a x)").bitcast(F32)
            mwords = masked[i][:].rearrange("p a x -> p (a x)").bitcast(F32)
            for j in range(2):
                pt = pt_pool.tile([P, 4, P], F32, name="pt")
                banks[(i, j)] = pt
                rows = [(a2, j) if size == 2 else (2 * j + a2, 0) for a2 in range(2)]
                for a2, (a, t) in enumerate(rows):
                    c0 = 256 * (4 * a + nr * tau + t)
                    nc.tensor.transpose(pt[:, 2 * a2 + 1 - u, :], words[:, c0 + 1 - u : c0 + 256 : 2], ident[:])
                for a2, (a, t) in enumerate(rows):
                    c0 = 128 * (nr * a + t)
                    nc.tensor.transpose(pt[:, 2 * a2 + u, :], mwords[:, c0 : c0 + 128], ident[:])

        def exits(i):
            size = tiles[ticks[i][0]][1]
            gt = g_pool.tile([P, 4 * N], BF16, name="grouped", align_bytes=64)
            grouped[i] = gt
            gw = gt[:].bitcast(F32).rearrange("p (t n k x) -> p t n k x", t=4 // size, k=size // 2, x=4)
            for j in range(2):
                t, k = (j, 0) if size == 2 else (0, j)
                nc.scalar.copy(out=gw[:, t, :, k, :], in_=banks[(i, j)][:].rearrange("q x n -> q n x"))

        def quantise_a(i):
            ac = c_pool.tile([P, N], U32, name="a_codes", align_bytes=64)
            sc = c_pool.tile([P, N], U8, name="a_scales", align_bytes=64)
            a_codes[i] = ac
            a_scales[i] = sc
            nc.vector.quantize_mx(out=ac[:].bitcast(FP8X4), scales=sc[:], in_=grouped[i][:])

        def multiply(i):
            b0, size = tiles[ticks[i][0]]
            po = po_pool.tile([P, 4, F], F32, name="po")
            o_ps[i] = po
            for k in range(4):
                b = b0 + k % size
                cols = slice(P * k, P * k + P)
                nc.tensor.matmul_mx(
                    out=po[:, k, :],
                    lhsT=a_codes[i][:, cols].bitcast(FP8X4),
                    lhsT_scale=a_scales[i][:, cols],
                    rhs=r_codes[b][:].bitcast(FP8X4),
                    rhs_scale=r_scales[b][:],
                    start=True,
                    stop=True,
                )

        def out_exit(i):
            z, tau = ticks[i]
            size = tiles[z][1]
            nr = 4 // size
            if tau == 0:
                o_sb[z] = o_pools[size].tile([P, size, 4, F], F32, name="o_sb")
            nc.scalar.copy(
                out=o_sb[z][:, :, nr * tau : nr * tau + nr, :],
                in_=o_ps[i][:].rearrange("m (t b) f -> m b t f", t=nr),
            )

        def store(z):
            b0, size = tiles[z]
            nc.sync.dma_start(
                out=out[b0 : b0 + size].rearrange("b (m r) f -> m b (r f)", r=4),
                in_=o_sb[z][:].rearrange("m b r f -> m b (r f)"),
            )

        needs = [(max(b0 - 1, -1), 0, z) for z, (b0, size) in enumerate(tiles)]
        needs.extend([(max(RB * k - 3, -1), 1, k) for k in range(B // RB)])
        loads = []
        seen = {2: [], 4: []}
        tick = -1
        for need, kind, idx in sorted(needs):
            if kind == 0:
                b0, size = tiles[idx]
                if len(seen[size]) >= ADJ_BUFS[size]:
                    old_b0, old_size = tiles[seen[size][len(seen[size]) - ADJ_BUFS[size]]]
                    tick = max(tick, old_b0 + old_size - 1)
                seen[size].append(idx)
            elif idx >= R_BUFS:
                tick = max(tick, RB * (idx - R_BUFS))
            loads.append((kind, idx, tick))
        last_load_tick = tick

        def issue_loads(now):
            for kind, idx, when in loads:
                if when == now and kind == 0:
                    load_adj(idx)
                if when == now and kind == 1:
                    load_r(idx)

        issue_loads(-1)
        mask(0)
        for i in range(B + 2):
            if i + 1 < B:
                mask(i + 1)
            if 1 <= i < B + 1:
                quantise_a(i - 1)
            if i == 0:
                regroup_r(0)
                regroup_r(1)
                quantise_r(0)
                regroup_r(2)
                quantise_r(1)
            if i + 3 < B:
                regroup_r(i + 3)
            if i + 2 < B:
                quantise_r(i + 2)
            if i < B:
                transposes(i)
            if i >= 2:
                multiply(i - 2)
            if i < B:
                exits(i)
            if i >= 2:
                out_exit(i - 2)
            issue_loads(i)
            for z, (b0, size) in enumerate(tiles):
                if max(b0 + size + 1, last_load_tick) == i:
                    store(z)
